import numpy as np
import ml_dtypes


def mxq(x, axis, fmt="e4m3"):
    dtype, down = {"e4m3": (ml_dtypes.float8_e4m3fn, 7), "e5m2": (ml_dtypes.float8_e5m2, 14)}[fmt]
    v = np.moveaxis(np.asarray(x, np.float32).astype(ml_dtypes.bfloat16).astype(np.float64), axis, -1)
    blocks = v.reshape(v.shape[:-1] + (-1, 32))
    amax = np.abs(blocks).max(-1, keepdims=True)
    byte = np.maximum(np.where(amax > 0, np.frexp(amax)[1] - 1 + 127, 0) - down, 1)
    scale = np.exp2(byte - 127.0)
    codes = (blocks / scale).astype(np.float32).astype(dtype).astype(np.float64)
    return np.moveaxis((codes * scale).reshape(v.shape), -1, axis)


WIDE = False


def mx_kscale(k):
    if not WIDE:
        return np.ones(k)
    levels = np.array([10, -10, 5, -5, 0])
    a = np.random.permutation(np.resize(levels, k // 512 * 4)).reshape(k // 512, 4)
    idx = np.arange(k)
    return np.exp2(a[idx // 512, idx % 128 // 32])


BF16 = ml_dtypes.bfloat16


def bf(x):
    return np.asarray(x, np.float32).astype(BF16)


def f64(x):
    return np.asarray(x).astype(np.float64)


B, S, IN_F, OUT_F, GS = 1, 256, 16384, 512, 128
GPR = IN_F // GS
N_GROUPS = OUT_F * GPR


def group_kscale():
    u = np.unique(mx_kscale(IN_F))
    u = u[np.argsort(-np.abs(np.log2(u)), kind="stable")]
    return u[np.arange(GPR) % len(u)]


def setup_inputs():
    tg = group_kscale()
    s = np.repeat(tg, GS)
    tflat = np.tile(tg, OUT_F)
    lo, hi = 0.64 / np.sqrt(IN_F), 3.2 / np.sqrt(IN_F)
    x = np.random.standard_normal((B, S, IN_F)) * s
    raw = np.random.standard_normal((OUT_F, IN_F))
    signs = np.where(raw >= 0, 1.0, -1.0)
    scale_pos = np.random.uniform(lo, hi, N_GROUPS) / tflat
    scale_neg = np.random.uniform(lo, hi, N_GROUPS) / tflat
    return {"x": bf(x), "signs": bf(signs), "scale_pos": bf(scale_pos), "scale_neg": bf(scale_neg), "gs": GS}


def reference(x, signs, scale_pos, scale_neg, gs):
    signs = f64(signs)
    out_f, in_f = signs.shape
    sp = np.repeat(f64(scale_pos), gs).reshape(out_f, in_f)
    sn = np.repeat(f64(scale_neg), gs).reshape(out_f, in_f)
    eff_scale = np.where(signs > 0, sp, sn)
    weight = signs * eff_scale
    return mxq(f64(x), 2, "e4m3") @ mxq(weight, 1, "e4m3").T

@@ -1,0 +1,203 @@
+from contextlib import ExitStack
+
+import concourse.mybir as mybir
+from concourse.masks import make_identity
+
+BF16 = mybir.dt.bfloat16
+F32 = mybir.dt.float32
+U32 = mybir.dt.uint32
+U8 = mybir.dt.uint8
+FP8X4 = mybir.dt.float8_e4m3fn_x4
+MULT = mybir.AluOpType.mult
+ADD = mybir.AluOpType.add
+SUBTRACT = mybir.AluOpType.subtract
+
+P = 128
+TOKENS = 256
+IN_F = 16384
+OUT_F = 512
+GROUP = 128
+GROUPS = IN_F // GROUP
+M_TILES = TOKENS // P
+O_TILES = OUT_F // P
+K_PASS = 4 * P
+N_PASS = IN_F // K_PASS
+GROUPS_PER_PASS = K_PASS // GROUP
+HALF = GROUP // 2
+CHUNK = 2048
+PASSES_PER_CHUNK = CHUNK // K_PASS
+N_CHUNKS = IN_F // CHUNK
+CHUNKS_IN_SBUF = 4
+QUANT_LAG = 2
+MX_LAG = 3
+
+FLOPS = 2 * TOKENS * IN_F * OUT_F
+
+
+def tile_signcondpackedbitlinear_k_kernel(tc, x, signs, scale_pos, scale_neg, gs, out):
+    nc = tc.nc
+    assert gs == GROUP
+    x_rows = x.flatten_outer_dims()
+    out_rows = out.flatten_outer_dims()
+
+    with ExitStack() as ctx:
+        const = ctx.enter_context(tc.tile_pool(name="const", bufs=1))
+        natural = ctx.enter_context(tc.tile_pool(name="natural", bufs=CHUNKS_IN_SBUF))
+        permuted = ctx.enter_context(tc.tile_pool(name="permuted", bufs=3))
+        grouped = ctx.enter_context(tc.tile_pool(name="grouped", bufs=4))
+        quantised = ctx.enter_context(tc.tile_pool(name="quantised", bufs=3))
+        results = ctx.enter_context(tc.tile_pool(name="results", bufs=1))
+        psum_acc = ctx.enter_context(tc.psum_pool(name="psum_acc", bufs=1))
+        psum_t = ctx.enter_context(tc.psum_pool(name="psum_t", bufs=6))
+
+        def load_chunk(i):
+            cols = slice(i * CHUNK, (i + 1) * CHUNK)
+            s_nat = []
+            for ot in range(O_TILES):
+                tile_s = natural.tile([P, CHUNK], BF16, name="s_nat%d" % ot)
+                nc.sync.dma_start(out=tile_s[:], in_=signs[ot * P : (ot + 1) * P, cols])
+                s_nat.append(tile_s)
+            x_nat = []
+            for mt in range(M_TILES):
+                tile_x = natural.tile([P, CHUNK], BF16, name="x_nat%d" % mt)
+                nc.sync.dma_start(out=tile_x[:], in_=x_rows[mt * P : (mt + 1) * P, cols])
+                x_nat.append(tile_x)
+            return s_nat, x_nat
+
+        pos = const.tile([P, O_TILES * GROUPS], BF16, name="pos")
+        neg = const.tile([P, O_TILES * GROUPS], BF16, name="neg")
+        nc.scalar.dma_start(
+            out=pos[:].rearrange("p (t g) -> p t g", t=O_TILES),
+            in_=scale_pos.rearrange("(t p g) -> p t g", t=O_TILES, p=P),
+        )
+        nc.scalar.dma_start(
+            out=neg[:].rearrange("p (t g) -> p t g", t=O_TILES),
+            in_=scale_neg.rearrange("(t p g) -> p t g", t=O_TILES, p=P),
+        )
+
+        chunks = {}
+        for i in range(CHUNKS_IN_SBUF):
+            chunks[i] = load_chunk(i)
+
+        ident = const.tile([P, P], F32, name="ident")
+        make_identity(nc, ident[:])
+
+        half_neg = const.tile([P, O_TILES * GROUPS], F32, name="half_neg")
+        slope = const.tile([P, O_TILES * GROUPS], F32, name="slope")
+        offset = const.tile([P, O_TILES * GROUPS], F32, name="offset")
+        nc.vector.tensor_scalar(out=half_neg[:], in0=neg[:], scalar1=0.5, scalar2=None, op0=MULT)
+        nc.vector.scalar_tensor_tensor(
+            out=slope[:], in0=pos[:], scalar=0.5, in1=half_neg[:], op0=MULT, op1=ADD
+        )
+        nc.vector.scalar_tensor_tensor(
+            out=offset[:], in0=pos[:], scalar=0.5, in1=half_neg[:], op0=MULT, op1=SUBTRACT
+        )
+
+        acc = [psum_acc.tile([P, OUT_F], F32, name="acc%d" % mt) for mt in range(M_TILES)]
+
+        def build_weight(c):
+            s_nat = chunks[c // PASSES_PER_CHUNK][0]
+            first = (c % PASSES_PER_CHUNK) * K_PASS
+            w_perm = permuted.tile([P, O_TILES * K_PASS], BF16, name="w_perm")
+            for ot in range(O_TILES):
+                dst = w_perm[:, ot * K_PASS : (ot + 1) * K_PASS].rearrange(
+                    "p (h j w) -> p h j w", h=2, j=GROUPS_PER_PASS
+                )
+                for j in range(GROUPS_PER_PASS):
+                    g = ot * GROUPS + c * GROUPS_PER_PASS + j
+                    src = s_nat[ot][:, first + j * GROUP : first + (j + 1) * GROUP]
+                    nc.vector.tensor_scalar(
+                        out=dst[:, :, j, :],
+                        in0=src.rearrange("p (h w) -> p h w", h=2),
+                        scalar1=slope[:, g : g + 1],
+                        scalar2=offset[:, g : g + 1],
+                        op0=MULT,
+                        op1=ADD,
+                    )
+            return w_perm
+
+        def permute_x(c):
+            x_nat = chunks[c // PASSES_PER_CHUNK][1]
+            first = (c % PASSES_PER_CHUNK) * K_PASS
+            x_perm = permuted.tile([P, M_TILES * K_PASS], BF16, name="x_perm")
+            for mt in range(M_TILES):
+                nc.vector.tensor_copy(
+                    out=x_perm[:, mt * K_PASS : (mt + 1) * K_PASS].rearrange(
+                        "p (h j w) -> p h j w", h=2, j=GROUPS_PER_PASS
+                    ),
+                    in_=x_nat[mt][:, first : first + K_PASS].rearrange(
+                        "p (j h w) -> p h j w", j=GROUPS_PER_PASS, h=2
+                    ),
+                )
+            return x_perm
+
+        def transpose_and_group(perm, row_tiles, name):
+            words = perm[:].bitcast(F32)
+            group_tile = grouped.tile([P, row_tiles * P * 4], BF16, name=name, align_bytes=64)
+            group_words = group_tile[:].bitcast(F32)
+            for pair in range(row_tiles // 2):
+                bank = psum_t.tile([P, 2, 2 * P], F32, name="bank")
+                for i in range(2):
+                    for h in range(2):
+                        col = ((2 * pair + i) * 2 + h) * P
+                        nc.tensor.transpose(
+                            bank[:, h, i * P : (i + 1) * P], words[:, col : col + P], ident[:]
+                        )
+                nc.scalar.copy(
+                    out=group_words[:, pair * 4 * P : (pair + 1) * 4 * P].rearrange(
+                        "p (n h) -> p n h", h=2
+                    ),
+                    in_=bank[:].rearrange("p h n -> p n h"),
+                )
+            return group_tile
+
+        def quantise(group_tile, columns, name):
+            codes = quantised.tile([P, columns], U32, name=name + "_codes", align_bytes=64)
+            scales = quantised.tile([P, columns], U8, name=name + "_scales", align_bytes=64)
+            nc.vector.quantize_mx(out=codes[:].bitcast(FP8X4), scales=scales[:], in_=group_tile[:])
+            return codes, scales
+
+        def multiply(c, x_q, w_q):
+            for mt in range(M_TILES):
+                rows = slice(mt * P, (mt + 1) * P)
+                nc.tensor.matmul_mx(
+                    out=acc[mt][:],
+                    lhsT=x_q[0][:, rows].bitcast(FP8X4),
+                    lhsT_scale=x_q[1][:, rows],
+                    rhs=w_q[0][:].bitcast(FP8X4),
+                    rhs_scale=w_q[1][:],
+                    start=(c == 0),
+                    stop=(c == N_PASS - 1),
+                )
+
+        in_groups = {}
+        in_codes = {}
+        for step in range(N_PASS + MX_LAG):
+            m = step - MX_LAG
+            if m >= 0:
+                multiply(m, in_codes[m][0], in_codes[m][1])
+            if step < N_PASS:
+                if step % PASSES_PER_CHUNK == 0:
+                    following = step // PASSES_PER_CHUNK - 1 + CHUNKS_IN_SBUF
+                    if CHUNKS_IN_SBUF <= following < N_CHUNKS:
+                        chunks[following] = load_chunk(following)
+                w_perm = build_weight(step)
+                x_perm = permute_x(step)
+                in_groups[step] = (
+                    transpose_and_group(x_perm, M_TILES, "x_group"),
+                    transpose_and_group(w_perm, O_TILES, "w_group"),
+                )
+            q = step - QUANT_LAG
+            if 0 <= q < N_PASS:
+                in_codes[q] = (
+                    quantise(in_groups[q][0], TOKENS, "x"),
+                    quantise(in_groups[q][1], OUT_F, "w"),
+                )
+
+        for mt in range(M_TILES):
+            result = results.tile([P, OUT_F], F32, name="result%d" % mt)
+            if mt == 0:
+                nc.vector.tensor_copy(out=result[:], in_=acc[mt][:])
+            else:
+                nc.scalar.copy(out=result[:], in_=acc[mt][:])
+            nc.sync.dma_start(out=out_rows[mt * P : (mt + 1) * P, :], in_=result[:])

@@ -28,8 +28,8 @@ CHUNK = 2048
 PASSES_PER_CHUNK = CHUNK // K_PASS
 N_CHUNKS = IN_F // CHUNK
 CHUNKS_IN_SBUF = 4
-QUANT_LAG = 2
-MX_LAG = 3
+QUANT_LAG = 1
+MX_LAG = 2
 
 FLOPS = 2 * TOKENS * IN_F * OUT_F
 
@@ -44,40 +44,40 @@ def tile_signcondpackedbitlinear_k_kernel(tc, x, signs, scale_pos, scale_neg, gs
         const = ctx.enter_context(tc.tile_pool(name="const", bufs=1))
         natural = ctx.enter_context(tc.tile_pool(name="natural", bufs=CHUNKS_IN_SBUF))
         permuted = ctx.enter_context(tc.tile_pool(name="permuted", bufs=3))
-        grouped = ctx.enter_context(tc.tile_pool(name="grouped", bufs=4))
+        grouped = ctx.enter_context(tc.tile_pool(name="grouped", bufs=3))
         quantised = ctx.enter_context(tc.tile_pool(name="quantised", bufs=3))
         results = ctx.enter_context(tc.tile_pool(name="results", bufs=1))
         psum_acc = ctx.enter_context(tc.psum_pool(name="psum_acc", bufs=1))
         psum_t = ctx.enter_context(tc.psum_pool(name="psum_t", bufs=6))
+        ctx.enter_context(tc.manual_schedule())
 
-        def load_chunk(i):
-            cols = slice(i * CHUNK, (i + 1) * CHUNK)
-            s_nat = []
-            for ot in range(O_TILES):
-                tile_s = natural.tile([P, CHUNK], BF16, name="s_nat%d" % ot)
-                nc.sync.dma_start(out=tile_s[:], in_=signs[ot * P : (ot + 1) * P, cols])
-                s_nat.append(tile_s)
-            x_nat = []
-            for mt in range(M_TILES):
-                tile_x = natural.tile([P, CHUNK], BF16, name="x_nat%d" % mt)
-                nc.sync.dma_start(out=tile_x[:], in_=x_rows[mt * P : (mt + 1) * P, cols])
-                x_nat.append(tile_x)
+        def load_chunk(i, pieces):
+            x_nat = [natural.tile([P, CHUNK], BF16, name="x_nat%d" % mt) for mt in range(M_TILES)]
+            s_nat = [natural.tile([P, CHUNK], BF16, name="s_nat%d" % ot) for ot in range(O_TILES)]
+            width = CHUNK // pieces
+            for piece in range(pieces):
+                here = slice(piece * width, (piece + 1) * width)
+                there = slice(i * CHUNK + piece * width, i * CHUNK + (piece + 1) * width)
+                for mt in range(M_TILES):
+                    nc.sync.dma_start(out=x_nat[mt][:, here], in_=x_rows[mt * P : (mt + 1) * P, there])
+                for ot in range(O_TILES):
+                    nc.sync.dma_start(out=s_nat[ot][:, here], in_=signs[ot * P : (ot + 1) * P, there])
             return s_nat, x_nat
 
         pos = const.tile([P, O_TILES * GROUPS], BF16, name="pos")
         neg = const.tile([P, O_TILES * GROUPS], BF16, name="neg")
-        nc.scalar.dma_start(
+        nc.sync.dma_start(
             out=pos[:].rearrange("p (t g) -> p t g", t=O_TILES),
             in_=scale_pos.rearrange("(t p g) -> p t g", t=O_TILES, p=P),
         )
-        nc.scalar.dma_start(
+        nc.sync.dma_start(
             out=neg[:].rearrange("p (t g) -> p t g", t=O_TILES),
             in_=scale_neg.rearrange("(t p g) -> p t g", t=O_TILES, p=P),
         )
 
         chunks = {}
         for i in range(CHUNKS_IN_SBUF):
-            chunks[i] = load_chunk(i)
+            chunks[i] = load_chunk(i, PASSES_PER_CHUNK if i == 0 else 1)
 
         ident = const.tile([P, P], F32, name="ident")
         make_identity(nc, ident[:])
@@ -173,20 +173,20 @@ def tile_signcondpackedbitlinear_k_kernel(tc, x, signs, scale_pos, scale_neg, gs
         in_groups = {}
         in_codes = {}
         for step in range(N_PASS + MX_LAG):
-            m = step - MX_LAG
-            if m >= 0:
-                multiply(m, in_codes[m][0], in_codes[m][1])
             if step < N_PASS:
                 if step % PASSES_PER_CHUNK == 0:
                     following = step // PASSES_PER_CHUNK - 1 + CHUNKS_IN_SBUF
                     if CHUNKS_IN_SBUF <= following < N_CHUNKS:
-                        chunks[following] = load_chunk(following)
-                w_perm = build_weight(step)
+                        chunks[following] = load_chunk(following, 1)
                 x_perm = permute_x(step)
+                w_perm = build_weight(step)
                 in_groups[step] = (
                     transpose_and_group(x_perm, M_TILES, "x_group"),
                     transpose_and_group(w_perm, O_TILES, "w_group"),
                 )
+            m = step - MX_LAG
+            if m >= 0:
+                multiply(m, in_codes[m][0], in_codes[m][1])
             q = step - QUANT_LAG
             if 0 <= q < N_PASS:
                 in_codes[q] = (

@@ -24,12 +24,12 @@ K_PASS = 4 * P
 N_PASS = IN_F // K_PASS
 GROUPS_PER_PASS = K_PASS // GROUP
 HALF = GROUP // 2
-CHUNK = 2048
+CHUNK = 1024
 PASSES_PER_CHUNK = CHUNK // K_PASS
 N_CHUNKS = IN_F // CHUNK
-CHUNKS_IN_SBUF = 4
-QUANT_LAG = 1
-MX_LAG = 2
+CHUNKS_IN_SBUF = 8
+QUANT_LAG = 2
+MX_LAG = 3
 
 FLOPS = 2 * TOKENS * IN_F * OUT_F
 
@@ -44,24 +44,24 @@ def tile_signcondpackedbitlinear_k_kernel(tc, x, signs, scale_pos, scale_neg, gs
         const = ctx.enter_context(tc.tile_pool(name="const", bufs=1))
         natural = ctx.enter_context(tc.tile_pool(name="natural", bufs=CHUNKS_IN_SBUF))
         permuted = ctx.enter_context(tc.tile_pool(name="permuted", bufs=3))
-        grouped = ctx.enter_context(tc.tile_pool(name="grouped", bufs=3))
+        grouped = ctx.enter_context(tc.tile_pool(name="grouped", bufs=4))
         quantised = ctx.enter_context(tc.tile_pool(name="quantised", bufs=3))
         results = ctx.enter_context(tc.tile_pool(name="results", bufs=1))
         psum_acc = ctx.enter_context(tc.psum_pool(name="psum_acc", bufs=1))
         psum_t = ctx.enter_context(tc.psum_pool(name="psum_t", bufs=6))
-        ctx.enter_context(tc.manual_schedule())
 
-        def load_chunk(i, pieces):
-            x_nat = [natural.tile([P, CHUNK], BF16, name="x_nat%d" % mt) for mt in range(M_TILES)]
-            s_nat = [natural.tile([P, CHUNK], BF16, name="s_nat%d" % ot) for ot in range(O_TILES)]
-            width = CHUNK // pieces
-            for piece in range(pieces):
-                here = slice(piece * width, (piece + 1) * width)
-                there = slice(i * CHUNK + piece * width, i * CHUNK + (piece + 1) * width)
-                for mt in range(M_TILES):
-                    nc.sync.dma_start(out=x_nat[mt][:, here], in_=x_rows[mt * P : (mt + 1) * P, there])
-                for ot in range(O_TILES):
-                    nc.sync.dma_start(out=s_nat[ot][:, here], in_=signs[ot * P : (ot + 1) * P, there])
+        def load_chunk(i):
+            cols = slice(i * CHUNK, (i + 1) * CHUNK)
+            x_nat = []
+            for mt in range(M_TILES):
+                tile_x = natural.tile([P, CHUNK], BF16, name="x_nat%d" % mt)
+                nc.sync.dma_start(out=tile_x[:], in_=x_rows[mt * P : (mt + 1) * P, cols])
+                x_nat.append(tile_x)
+            s_nat = []
+            for ot in range(O_TILES):
+                tile_s = natural.tile([P, CHUNK], BF16, name="s_nat%d" % ot)
+                nc.sync.dma_start(out=tile_s[:], in_=signs[ot * P : (ot + 1) * P, cols])
+                s_nat.append(tile_s)
             return s_nat, x_nat
 
         pos = const.tile([P, O_TILES * GROUPS], BF16, name="pos")
@@ -77,7 +77,7 @@ def tile_signcondpackedbitlinear_k_kernel(tc, x, signs, scale_pos, scale_neg, gs
 
         chunks = {}
         for i in range(CHUNKS_IN_SBUF):
-            chunks[i] = load_chunk(i, PASSES_PER_CHUNK if i == 0 else 1)
+            chunks[i] = load_chunk(i)
 
         ident = const.tile([P, P], F32, name="ident")
         make_identity(nc, ident[:])
@@ -120,15 +120,20 @@ def tile_signcondpackedbitlinear_k_kernel(tc, x, signs, scale_pos, scale_neg, gs
             x_nat = chunks[c // PASSES_PER_CHUNK][1]
             first = (c % PASSES_PER_CHUNK) * K_PASS
             x_perm = permuted.tile([P, M_TILES * K_PASS], BF16, name="x_perm")
-            for mt in range(M_TILES):
-                nc.vector.tensor_copy(
-                    out=x_perm[:, mt * K_PASS : (mt + 1) * K_PASS].rearrange(
-                        "p (h j w) -> p h j w", h=2, j=GROUPS_PER_PASS
-                    ),
-                    in_=x_nat[mt][:, first : first + K_PASS].rearrange(
-                        "p (j h w) -> p h j w", j=GROUPS_PER_PASS, h=2
-                    ),
-                )
+            nc.vector.tensor_copy(
+                out=x_perm[:, 0:K_PASS].rearrange("p (h j w) -> p h j w", h=2, j=GROUPS_PER_PASS),
+                in_=x_nat[0][:, first : first + K_PASS].rearrange(
+                    "p (j h w) -> p h j w", j=GROUPS_PER_PASS, h=2
+                ),
+            )
+            nc.scalar.copy(
+                out=x_perm[:, K_PASS : 2 * K_PASS]
+                .bitcast(F32)
+                .rearrange("p (h j w) -> p h j w", h=2, j=GROUPS_PER_PASS),
+                in_=x_nat[1][:, first : first + K_PASS]
+                .bitcast(F32)
+                .rearrange("p (j h w) -> p h j w", j=GROUPS_PER_PASS, h=2),
+            )
             return x_perm
 
         def transpose_and_group(perm, row_tiles, name):
@@ -173,20 +178,20 @@ def tile_signcondpackedbitlinear_k_kernel(tc, x, signs, scale_pos, scale_neg, gs
         in_groups = {}
         in_codes = {}
         for step in range(N_PASS + MX_LAG):
+            m = step - MX_LAG
+            if m >= 0:
+                multiply(m, in_codes[m][0], in_codes[m][1])
             if step < N_PASS:
                 if step % PASSES_PER_CHUNK == 0:
                     following = step // PASSES_PER_CHUNK - 1 + CHUNKS_IN_SBUF
                     if CHUNKS_IN_SBUF <= following < N_CHUNKS:
-                        chunks[following] = load_chunk(following, 1)
-                x_perm = permute_x(step)
+                        chunks[following] = load_chunk(following)
                 w_perm = build_weight(step)
+                x_perm = permute_x(step)
                 in_groups[step] = (
                     transpose_and_group(x_perm, M_TILES, "x_group"),
                     transpose_and_group(w_perm, O_TILES, "w_group"),
                 )
-            m = step - MX_LAG
-            if m >= 0:
-                multiply(m, in_codes[m][0], in_codes[m][1])
             q = step - QUANT_LAG
             if 0 <= q < N_PASS:
                 in_codes[q] = (

@@ -24,10 +24,10 @@ K_PASS = 4 * P
 N_PASS = IN_F // K_PASS
 GROUPS_PER_PASS = K_PASS // GROUP
 HALF = GROUP // 2
-CHUNK = 1024
-PASSES_PER_CHUNK = CHUNK // K_PASS
-N_CHUNKS = IN_F // CHUNK
-CHUNKS_IN_SBUF = 8
+CHUNKS = (512, 512, 1024, 2048, 4096, 4096, 2048, 1024, 512, 512)
+CHUNKS_AT_START = 6
+BUFFERS = {512: 2, 1024: 1, 2048: 1, 4096: 2}
+REUSE_STEP = 8
 QUANT_LAG = 2
 MX_LAG = 3
 
@@ -42,7 +42,7 @@ def tile_signcondpackedbitlinear_k_kernel(tc, x, signs, scale_pos, scale_neg, gs
 
     with ExitStack() as ctx:
         const = ctx.enter_context(tc.tile_pool(name="const", bufs=1))
-        natural = ctx.enter_context(tc.tile_pool(name="natural", bufs=CHUNKS_IN_SBUF))
+        natural = ctx.enter_context(tc.tile_pool(name="natural", bufs=1))
         permuted = ctx.enter_context(tc.tile_pool(name="permuted", bufs=3))
         grouped = ctx.enter_context(tc.tile_pool(name="grouped", bufs=4))
         quantised = ctx.enter_context(tc.tile_pool(name="quantised", bufs=3))
@@ -50,18 +50,23 @@ def tile_signcondpackedbitlinear_k_kernel(tc, x, signs, scale_pos, scale_neg, gs
         psum_acc = ctx.enter_context(tc.psum_pool(name="psum_acc", bufs=1))
         psum_t = ctx.enter_context(tc.psum_pool(name="psum_t", bufs=6))
 
+        chunk_of_pass = []
+
         def load_chunk(i):
-            cols = slice(i * CHUNK, (i + 1) * CHUNK)
+            width = CHUNKS[i]
+            cols = slice(sum(CHUNKS[:i]), sum(CHUNKS[: i + 1]))
             x_nat = []
             for mt in range(M_TILES):
-                tile_x = natural.tile([P, CHUNK], BF16, name="x_nat%d" % mt)
+                tile_x = natural.tile([P, width], BF16, name="x%d_%d" % (mt, width), bufs=BUFFERS[width])
                 nc.sync.dma_start(out=tile_x[:], in_=x_rows[mt * P : (mt + 1) * P, cols])
                 x_nat.append(tile_x)
             s_nat = []
             for ot in range(O_TILES):
-                tile_s = natural.tile([P, CHUNK], BF16, name="s_nat%d" % ot)
+                tile_s = natural.tile([P, width], BF16, name="s%d_%d" % (ot, width), bufs=BUFFERS[width])
                 nc.sync.dma_start(out=tile_s[:], in_=signs[ot * P : (ot + 1) * P, cols])
                 s_nat.append(tile_s)
+            for c in range(width // K_PASS):
+                chunk_of_pass.append((i, c * K_PASS))
             return s_nat, x_nat
 
         pos = const.tile([P, O_TILES * GROUPS], BF16, name="pos")
@@ -76,7 +81,7 @@ def tile_signcondpackedbitlinear_k_kernel(tc, x, signs, scale_pos, scale_neg, gs
         )
 
         chunks = {}
-        for i in range(CHUNKS_IN_SBUF):
+        for i in range(CHUNKS_AT_START):
             chunks[i] = load_chunk(i)
 
         ident = const.tile([P, P], F32, name="ident")
@@ -96,8 +101,8 @@ def tile_signcondpackedbitlinear_k_kernel(tc, x, signs, scale_pos, scale_neg, gs
         acc = [psum_acc.tile([P, OUT_F], F32, name="acc%d" % mt) for mt in range(M_TILES)]
 
         def build_weight(c):
-            s_nat = chunks[c // PASSES_PER_CHUNK][0]
-            first = (c % PASSES_PER_CHUNK) * K_PASS
+            chunk, first = chunk_of_pass[c]
+            s_nat = chunks[chunk][0]
             w_perm = permuted.tile([P, O_TILES * K_PASS], BF16, name="w_perm")
             for ot in range(O_TILES):
                 dst = w_perm[:, ot * K_PASS : (ot + 1) * K_PASS].rearrange(
@@ -117,8 +122,8 @@ def tile_signcondpackedbitlinear_k_kernel(tc, x, signs, scale_pos, scale_neg, gs
             return w_perm
 
         def permute_x(c):
-            x_nat = chunks[c // PASSES_PER_CHUNK][1]
-            first = (c % PASSES_PER_CHUNK) * K_PASS
+            chunk, first = chunk_of_pass[c]
+            x_nat = chunks[chunk][1]
             x_perm = permuted.tile([P, M_TILES * K_PASS], BF16, name="x_perm")
             nc.vector.tensor_copy(
                 out=x_perm[:, 0:K_PASS].rearrange("p (h j w) -> p h j w", h=2, j=GROUPS_PER_PASS),
@@ -182,10 +187,9 @@ def tile_signcondpackedbitlinear_k_kernel(tc, x, signs, scale_pos, scale_neg, gs
             if m >= 0:
                 multiply(m, in_codes[m][0], in_codes[m][1])
             if step < N_PASS:
-                if step % PASSES_PER_CHUNK == 0:
-                    following = step // PASSES_PER_CHUNK - 1 + CHUNKS_IN_SBUF
-                    if CHUNKS_IN_SBUF <= following < N_CHUNKS:
-                        chunks[following] = load_chunk(following)
+                if step == REUSE_STEP:
+                    for i in range(CHUNKS_AT_START, len(CHUNKS)):
+                        chunks[i] = load_chunk(i)
                 w_perm = build_weight(step)
                 x_perm = permute_x(step)
                 in_groups[step] = (

@@ -23,13 +23,10 @@ O_TILES = OUT_F // P
 K_PASS = 4 * P
 N_PASS = IN_F // K_PASS
 GROUPS_PER_PASS = K_PASS // GROUP
-HALF = GROUP // 2
-CHUNKS = (512, 512, 1024, 2048, 4096, 4096, 2048, 1024, 512, 512)
-CHUNKS_AT_START = 6
-BUFFERS = {512: 2, 1024: 1, 2048: 1, 4096: 2}
-REUSE_STEP = 8
-QUANT_LAG = 2
-MX_LAG = 3
+CHUNKS = (512, 512) + 14 * (1024,) + (512, 512)
+BUFFERS = {512: 2, 1024: 8}
+CHUNKS_AT_START = 10
+MX_BATCH = 2
 
 FLOPS = 2 * TOKENS * IN_F * OUT_F
 
@@ -45,12 +42,13 @@ def tile_signcondpackedbitlinear_k_kernel(tc, x, signs, scale_pos, scale_neg, gs
         natural = ctx.enter_context(tc.tile_pool(name="natural", bufs=1))
         permuted = ctx.enter_context(tc.tile_pool(name="permuted", bufs=3))
         grouped = ctx.enter_context(tc.tile_pool(name="grouped", bufs=4))
-        quantised = ctx.enter_context(tc.tile_pool(name="quantised", bufs=3))
+        quantised = ctx.enter_context(tc.tile_pool(name="quantised", bufs=5))
         results = ctx.enter_context(tc.tile_pool(name="results", bufs=1))
         psum_acc = ctx.enter_context(tc.psum_pool(name="psum_acc", bufs=1))
         psum_t = ctx.enter_context(tc.psum_pool(name="psum_t", bufs=6))
 
         chunk_of_pass = []
+        chunks = {}
 
         def load_chunk(i):
             width = CHUNKS[i]
@@ -67,7 +65,7 @@ def tile_signcondpackedbitlinear_k_kernel(tc, x, signs, scale_pos, scale_neg, gs
                 s_nat.append(tile_s)
             for c in range(width // K_PASS):
                 chunk_of_pass.append((i, c * K_PASS))
-            return s_nat, x_nat
+            chunks[i] = (s_nat, x_nat)
 
         pos = const.tile([P, O_TILES * GROUPS], BF16, name="pos")
         neg = const.tile([P, O_TILES * GROUPS], BF16, name="neg")
@@ -80,9 +78,8 @@ def tile_signcondpackedbitlinear_k_kernel(tc, x, signs, scale_pos, scale_neg, gs
             in_=scale_neg.rearrange("(t p g) -> p t g", t=O_TILES, p=P),
         )
 
-        chunks = {}
         for i in range(CHUNKS_AT_START):
-            chunks[i] = load_chunk(i)
+            load_chunk(i)
 
         ident = const.tile([P, P], F32, name="ident")
         make_identity(nc, ident[:])
@@ -99,6 +96,9 @@ def tile_signcondpackedbitlinear_k_kernel(tc, x, signs, scale_pos, scale_neg, gs
         )
 
         acc = [psum_acc.tile([P, OUT_F], F32, name="acc%d" % mt) for mt in range(M_TILES)]
+        w_perms = {}
+        groups = {}
+        codes = {}
 
         def build_weight(c):
             chunk, first = chunk_of_pass[c]
@@ -112,40 +112,36 @@ def tile_signcondpackedbitlinear_k_kernel(tc, x, signs, scale_pos, scale_neg, gs
                     g = ot * GROUPS + c * GROUPS_PER_PASS + j
                     src = s_nat[ot][:, first + j * GROUP : first + (j + 1) * GROUP]
                     nc.vector.tensor_scalar(
-                        out=dst[:, :, j, :],
-                        in0=src.rearrange("p (h w) -> p h w", h=2),
+                        out=dst[:, :, j, :].rearrange("p h (w e) -> p h w e", e=2),
+                        in0=src.rearrange("p (w h e) -> p h w e", h=2, e=2),
                         scalar1=slope[:, g : g + 1],
                         scalar2=offset[:, g : g + 1],
                         op0=MULT,
                         op1=ADD,
                     )
-            return w_perm
+            w_perms[c] = w_perm
 
-        def permute_x(c):
+        def transpose_x(c):
             chunk, first = chunk_of_pass[c]
-            x_nat = chunks[chunk][1]
-            x_perm = permuted.tile([P, M_TILES * K_PASS], BF16, name="x_perm")
-            nc.vector.tensor_copy(
-                out=x_perm[:, 0:K_PASS].rearrange("p (h j w) -> p h j w", h=2, j=GROUPS_PER_PASS),
-                in_=x_nat[0][:, first : first + K_PASS].rearrange(
-                    "p (j h w) -> p h j w", j=GROUPS_PER_PASS, h=2
-                ),
-            )
+            x_group = grouped.tile([P, M_TILES * P * 4], BF16, name="x_group", align_bytes=64)
+            bank = psum_t.tile([P, 2, 2 * P], F32, name="bank")
+            for mt in range(M_TILES):
+                words = chunks[chunk][1][mt][:, first : first + K_PASS].bitcast(F32)
+                for h in range(2):
+                    nc.tensor.transpose(
+                        bank[:, h, mt * P : (mt + 1) * P], words[:, h : 2 * P : 2], ident[:]
+                    )
             nc.scalar.copy(
-                out=x_perm[:, K_PASS : 2 * K_PASS]
-                .bitcast(F32)
-                .rearrange("p (h j w) -> p h j w", h=2, j=GROUPS_PER_PASS),
-                in_=x_nat[1][:, first : first + K_PASS]
-                .bitcast(F32)
-                .rearrange("p (j h w) -> p h j w", j=GROUPS_PER_PASS, h=2),
+                out=x_group[:].bitcast(F32).rearrange("p (n h) -> p n h", h=2),
+                in_=bank[:].rearrange("p h n -> p n h"),
             )
-            return x_perm
+            groups[c] = [x_group]
 
-        def transpose_and_group(perm, row_tiles, name):
-            words = perm[:].bitcast(F32)
-            group_tile = grouped.tile([P, row_tiles * P * 4], BF16, name=name, align_bytes=64)
-            group_words = group_tile[:].bitcast(F32)
-            for pair in range(row_tiles // 2):
+        def transpose_w(c):
+            words = w_perms[c][:].bitcast(F32)
+            w_group = grouped.tile([P, O_TILES * P * 4], BF16, name="w_group", align_bytes=64)
+            group_words = w_group[:].bitcast(F32)
+            for pair in range(O_TILES // 2):
                 bank = psum_t.tile([P, 2, 2 * P], F32, name="bank")
                 for i in range(2):
                     for h in range(2):
@@ -159,15 +155,19 @@ def tile_signcondpackedbitlinear_k_kernel(tc, x, signs, scale_pos, scale_neg, gs
                     ),
                     in_=bank[:].rearrange("p h n -> p n h"),
                 )
-            return group_tile
+            groups[c].append(w_group)
 
-        def quantise(group_tile, columns, name):
-            codes = quantised.tile([P, columns], U32, name=name + "_codes", align_bytes=64)
-            scales = quantised.tile([P, columns], U8, name=name + "_scales", align_bytes=64)
-            nc.vector.quantize_mx(out=codes[:].bitcast(FP8X4), scales=scales[:], in_=group_tile[:])
-            return codes, scales
+        def quantise(c):
+            made = []
+            for group_tile, columns, name in zip(groups[c], (TOKENS, OUT_F), ("x", "w")):
+                code = quantised.tile([P, columns], U32, name=name + "_codes", align_bytes=64)
+                scale = quantised.tile([P, columns], U8, name=name + "_scales", align_bytes=64)
+                nc.vector.quantize_mx(out=code[:].bitcast(FP8X4), scales=scale[:], in_=group_tile[:])
+                made.append((code, scale))
+            codes[c] = made
 
-        def multiply(c, x_q, w_q):
+        def multiply(c):
+            x_q, w_q = codes[c]
             for mt in range(M_TILES):
                 rows = slice(mt * P, (mt + 1) * P)
                 nc.tensor.matmul_mx(
@@ -180,28 +180,25 @@ def tile_signcondpackedbitlinear_k_kernel(tc, x, signs, scale_pos, scale_neg, gs
                     stop=(c == N_PASS - 1),
                 )
 
-        in_groups = {}
-        in_codes = {}
-        for step in range(N_PASS + MX_LAG):
-            m = step - MX_LAG
-            if m >= 0:
-                multiply(m, in_codes[m][0], in_codes[m][1])
+        ctx.enter_context(tc.manual_schedule())
+        multiplied = 0
+        free_step = {512: [2, 2], 1024: list(range(4, N_PASS, 2))}
+        for step in range(N_PASS + 3):
+            while len(chunks) < len(CHUNKS) and free_step[CHUNKS[len(chunks)]][0] <= step:
+                free_step[CHUNKS[len(chunks)]].pop(0)
+                load_chunk(len(chunks))
             if step < N_PASS:
-                if step == REUSE_STEP:
-                    for i in range(CHUNKS_AT_START, len(CHUNKS)):
-                        chunks[i] = load_chunk(i)
-                w_perm = build_weight(step)
-                x_perm = permute_x(step)
-                in_groups[step] = (
-                    transpose_and_group(x_perm, M_TILES, "x_group"),
-                    transpose_and_group(w_perm, O_TILES, "w_group"),
-                )
-            q = step - QUANT_LAG
-            if 0 <= q < N_PASS:
-                in_codes[q] = (
-                    quantise(in_groups[q][0], TOKENS, "x"),
-                    quantise(in_groups[q][1], OUT_F, "w"),
-                )
+                transpose_x(step)
+            if 0 <= step - 1 < N_PASS:
+                transpose_w(step - 1)
+            if step % MX_BATCH == 0 or step >= N_PASS:
+                while multiplied <= step - 3:
+                    multiply(multiplied)
+                    multiplied += 1
+            if step < N_PASS:
+                build_weight(step)
+            if 0 <= step - 2 < N_PASS:
+                quantise(step - 2)
 
         for mt in range(M_TILES):
             result = results.tile([P, OUT_F], F32, name="result%d" % mt)

@@ -26,7 +26,7 @@ GROUPS_PER_PASS = K_PASS // GROUP
 CHUNKS = (512, 512) + 14 * (1024,) + (512, 512)
 BUFFERS = {512: 2, 1024: 8}
 CHUNKS_AT_START = 10
-MX_BATCH = 2
+MX_BATCH = 1
 
 FLOPS = 2 * TOKENS * IN_F * OUT_F
 

@@ -23,10 +23,14 @@ O_TILES = OUT_F // P
 K_PASS = 4 * P
 N_PASS = IN_F // K_PASS
 GROUPS_PER_PASS = K_PASS // GROUP
-CHUNKS = (512, 512) + 14 * (1024,) + (512, 512)
-BUFFERS = {512: 2, 1024: 8}
-CHUNKS_AT_START = 10
-MX_BATCH = 1
+CHUNKS = 16 * (1024,)
+CHUNKS_IN_SBUF = 9
+MX_LAG = 0
+PERMUTE_LEAD = 2
+QUANT_LAG = 4
+PAIRS = 1 + O_TILES // 2
+PAIR_ORDER = (1, 0, 2)
+LOAD_ORDER = (2, 3, 0, 1, 4, 5)
 
 FLOPS = 2 * TOKENS * IN_F * OUT_F
 
@@ -36,50 +40,48 @@ def tile_signcondpackedbitlinear_k_kernel(tc, x, signs, scale_pos, scale_neg, gs
     assert gs == GROUP
     x_rows = x.flatten_outer_dims()
     out_rows = out.flatten_outer_dims()
+    sign_rows = signs.rearrange("(p t) k -> p t k", t=O_TILES)
 
     with ExitStack() as ctx:
         const = ctx.enter_context(tc.tile_pool(name="const", bufs=1))
-        natural = ctx.enter_context(tc.tile_pool(name="natural", bufs=1))
-        permuted = ctx.enter_context(tc.tile_pool(name="permuted", bufs=3))
-        grouped = ctx.enter_context(tc.tile_pool(name="grouped", bufs=4))
-        quantised = ctx.enter_context(tc.tile_pool(name="quantised", bufs=5))
+        natural = ctx.enter_context(tc.tile_pool(name="natural", bufs=CHUNKS_IN_SBUF))
+        permuted = ctx.enter_context(tc.tile_pool(name="permuted", bufs=8))
+        grouped = ctx.enter_context(tc.tile_pool(name="grouped", bufs=8))
+        quantised = ctx.enter_context(tc.tile_pool(name="quantised", bufs=8))
         results = ctx.enter_context(tc.tile_pool(name="results", bufs=1))
         psum_acc = ctx.enter_context(tc.psum_pool(name="psum_acc", bufs=1))
         psum_t = ctx.enter_context(tc.psum_pool(name="psum_t", bufs=6))
 
+        items = []
         chunk_of_pass = []
-        chunks = {}
+        for i, width in enumerate(CHUNKS):
+            first_pass = sum(CHUNKS[:i]) // K_PASS
+            passes = range(first_pass, first_pass + width // K_PASS)
+            items.extend((c, pair) for pair in PAIR_ORDER for c in passes)
+            chunk_of_pass.extend((i, (c - first_pass) * K_PASS) for c in passes)
+        chunks = []
 
-        def load_chunk(i):
-            width = CHUNKS[i]
+        def load_chunk():
+            i = len(chunks)
             cols = slice(sum(CHUNKS[:i]), sum(CHUNKS[: i + 1]))
-            x_nat = []
-            for mt in range(M_TILES):
-                tile_x = natural.tile([P, width], BF16, name="x%d_%d" % (mt, width), bufs=BUFFERS[width])
-                nc.sync.dma_start(out=tile_x[:], in_=x_rows[mt * P : (mt + 1) * P, cols])
-                x_nat.append(tile_x)
-            s_nat = []
-            for ot in range(O_TILES):
-                tile_s = natural.tile([P, width], BF16, name="s%d_%d" % (ot, width), bufs=BUFFERS[width])
-                nc.sync.dma_start(out=tile_s[:], in_=signs[ot * P : (ot + 1) * P, cols])
-                s_nat.append(tile_s)
-            for c in range(width // K_PASS):
-                chunk_of_pass.append((i, c * K_PASS))
-            chunks[i] = (s_nat, x_nat)
+            tiles = {}
+            for rt in LOAD_ORDER:
+                tile_n = natural.tile([P, CHUNKS[i]], BF16, name="natural%d" % rt)
+                if rt < M_TILES:
+                    rows = x_rows[rt * P : (rt + 1) * P, cols]
+                else:
+                    rows = sign_rows[:, rt - M_TILES, cols]
+                nc.sync.dma_start(out=tile_n[:], in_=rows)
+                tiles[rt] = tile_n
+            chunks.append(tiles)
 
         pos = const.tile([P, O_TILES * GROUPS], BF16, name="pos")
         neg = const.tile([P, O_TILES * GROUPS], BF16, name="neg")
-        nc.sync.dma_start(
-            out=pos[:].rearrange("p (t g) -> p t g", t=O_TILES),
-            in_=scale_pos.rearrange("(t p g) -> p t g", t=O_TILES, p=P),
-        )
-        nc.sync.dma_start(
-            out=neg[:].rearrange("p (t g) -> p t g", t=O_TILES),
-            in_=scale_neg.rearrange("(t p g) -> p t g", t=O_TILES, p=P),
-        )
+        nc.sync.dma_start(out=pos[:], in_=scale_pos.rearrange("(p c) -> p c", p=P))
+        nc.sync.dma_start(out=neg[:], in_=scale_neg.rearrange("(p c) -> p c", p=P))
 
-        for i in range(CHUNKS_AT_START):
-            load_chunk(i)
+        for i in range(CHUNKS_IN_SBUF):
+            load_chunk()
 
         ident = const.tile([P, P], F32, name="ident")
         make_identity(nc, ident[:])
@@ -87,30 +89,42 @@ def tile_signcondpackedbitlinear_k_kernel(tc, x, signs, scale_pos, scale_neg, gs
         half_neg = const.tile([P, O_TILES * GROUPS], F32, name="half_neg")
         slope = const.tile([P, O_TILES * GROUPS], F32, name="slope")
         offset = const.tile([P, O_TILES * GROUPS], F32, name="offset")
-        nc.vector.tensor_scalar(out=half_neg[:], in0=neg[:], scalar1=0.5, scalar2=None, op0=MULT)
-        nc.vector.scalar_tensor_tensor(
-            out=slope[:], in0=pos[:], scalar=0.5, in1=half_neg[:], op0=MULT, op1=ADD
-        )
-        nc.vector.scalar_tensor_tensor(
-            out=offset[:], in0=pos[:], scalar=0.5, in1=half_neg[:], op0=MULT, op1=SUBTRACT
-        )
+        for ot in range(O_TILES):
+            cols = slice(ot * GROUPS, (ot + 1) * GROUPS)
+            nc.vector.tensor_scalar(
+                out=half_neg[:, cols], in0=neg[:, cols], scalar1=0.5, scalar2=None, op0=MULT
+            )
+            nc.vector.scalar_tensor_tensor(
+                out=slope[:, cols], in0=pos[:, cols], scalar=0.5, in1=half_neg[:, cols], op0=MULT, op1=ADD
+            )
+            nc.vector.scalar_tensor_tensor(
+                out=offset[:, cols],
+                in0=pos[:, cols],
+                scalar=0.5,
+                in1=half_neg[:, cols],
+                op0=MULT,
+                op1=SUBTRACT,
+            )
 
         acc = [psum_acc.tile([P, OUT_F], F32, name="acc%d" % mt) for mt in range(M_TILES)]
+        x_perms = {}
         w_perms = {}
-        groups = {}
-        codes = {}
+        group_tiles = {}
+        x_q = {}
+        w_q = {}
 
-        def build_weight(c):
+        def build(c, pair):
             chunk, first = chunk_of_pass[c]
-            s_nat = chunks[chunk][0]
-            w_perm = permuted.tile([P, O_TILES * K_PASS], BF16, name="w_perm")
-            for ot in range(O_TILES):
-                dst = w_perm[:, ot * K_PASS : (ot + 1) * K_PASS].rearrange(
+            w_perm = permuted.tile([P, 2 * K_PASS], BF16, name="w_perm")
+            for i in range(2):
+                ot = 2 * (pair - 1) + i
+                src_tile = chunks[chunk][M_TILES + ot]
+                dst = w_perm[:, i * K_PASS : (i + 1) * K_PASS].rearrange(
                     "p (h j w) -> p h j w", h=2, j=GROUPS_PER_PASS
                 )
                 for j in range(GROUPS_PER_PASS):
                     g = ot * GROUPS + c * GROUPS_PER_PASS + j
-                    src = s_nat[ot][:, first + j * GROUP : first + (j + 1) * GROUP]
+                    src = src_tile[:, first + j * GROUP : first + (j + 1) * GROUP]
                     nc.vector.tensor_scalar(
                         out=dst[:, :, j, :].rearrange("p h (w e) -> p h w e", e=2),
                         in0=src.rearrange("p (w h e) -> p h w e", h=2, e=2),
@@ -119,91 +133,116 @@ def tile_signcondpackedbitlinear_k_kernel(tc, x, signs, scale_pos, scale_neg, gs
                         op0=MULT,
                         op1=ADD,
                     )
-            w_perms[c] = w_perm
+            w_perms[c, pair] = w_perm
 
-        def transpose_x(c):
+        def permute_x(c):
             chunk, first = chunk_of_pass[c]
-            x_group = grouped.tile([P, M_TILES * P * 4], BF16, name="x_group", align_bytes=64)
+            src = chunks[chunk][1][:, first : first + K_PASS]
+            x_perm = permuted.tile([P, K_PASS], BF16, name="x_perm")
+            if c % 2 == 0:
+                nc.vector.tensor_copy(
+                    out=x_perm[:].rearrange("p (h w e) -> p h w e", h=2, e=2),
+                    in_=src.rearrange("p (w h e) -> p h w e", h=2, e=2),
+                )
+            else:
+                nc.scalar.copy(
+                    out=x_perm[:].bitcast(F32).rearrange("p (h w) -> p h w", h=2),
+                    in_=src.bitcast(F32).rearrange("p (w h) -> p h w", h=2),
+                )
+            x_perms[c] = x_perm
+
+        def transpose(c, pair):
             bank = psum_t.tile([P, 2, 2 * P], F32, name="bank")
-            for mt in range(M_TILES):
-                words = chunks[chunk][1][mt][:, first : first + K_PASS].bitcast(F32)
+            for i in range(2):
                 for h in range(2):
-                    nc.tensor.transpose(
-                        bank[:, h, mt * P : (mt + 1) * P], words[:, h : 2 * P : 2], ident[:]
-                    )
+                    if pair == 0 and i == 0:
+                        chunk, first = chunk_of_pass[c]
+                        words = chunks[chunk][i][:, first : first + K_PASS].bitcast(F32)
+                        in_words = words[:, h : 2 * P : 2]
+                    elif pair == 0:
+                        in_words = x_perms[c][:].bitcast(F32)[:, h * P : (h + 1) * P]
+                    else:
+                        words = w_perms[c, pair][:].bitcast(F32)
+                        in_words = words[:, (2 * i + h) * P : (2 * i + h + 1) * P]
+                    nc.tensor.transpose(bank[:, h, i * P : (i + 1) * P], in_words, ident[:])
+            group_tile = grouped.tile([P, 2 * P * 4], BF16, name="group_tile", align_bytes=64)
             nc.scalar.copy(
-                out=x_group[:].bitcast(F32).rearrange("p (n h) -> p n h", h=2),
+                out=group_tile[:].bitcast(F32).rearrange("p (n h) -> p n h", h=2),
                 in_=bank[:].rearrange("p h n -> p n h"),
             )
-            groups[c] = [x_group]
+            group_tiles[c, pair] = group_tile
 
-        def transpose_w(c):
-            words = w_perms[c][:].bitcast(F32)
-            w_group = grouped.tile([P, O_TILES * P * 4], BF16, name="w_group", align_bytes=64)
-            group_words = w_group[:].bitcast(F32)
-            for pair in range(O_TILES // 2):
-                bank = psum_t.tile([P, 2, 2 * P], F32, name="bank")
-                for i in range(2):
-                    for h in range(2):
-                        col = ((2 * pair + i) * 2 + h) * P
-                        nc.tensor.transpose(
-                            bank[:, h, i * P : (i + 1) * P], words[:, col : col + P], ident[:]
-                        )
-                nc.scalar.copy(
-                    out=group_words[:, pair * 4 * P : (pair + 1) * 4 * P].rearrange(
-                        "p (n h) -> p n h", h=2
-                    ),
-                    in_=bank[:].rearrange("p h n -> p n h"),
-                )
-            groups[c].append(w_group)
-
-        def quantise(c):
-            made = []
-            for group_tile, columns, name in zip(groups[c], (TOKENS, OUT_F), ("x", "w")):
-                code = quantised.tile([P, columns], U32, name=name + "_codes", align_bytes=64)
-                scale = quantised.tile([P, columns], U8, name=name + "_scales", align_bytes=64)
-                nc.vector.quantize_mx(out=code[:].bitcast(FP8X4), scales=scale[:], in_=group_tile[:])
-                made.append((code, scale))
-            codes[c] = made
+        def quantise(c, pair):
+            if pair == 0:
+                x_codes = quantised.tile([P, TOKENS], U32, name="x_codes", align_bytes=64)
+                x_scales = quantised.tile([P, TOKENS], U8, name="x_scales", align_bytes=64)
+                x_q[c] = (x_codes, x_scales)
+                codes, scales = x_codes[:], x_scales[:]
+            else:
+                if c not in w_q:
+                    w_codes = quantised.tile([P, OUT_F], U32, name="w_codes", align_bytes=64)
+                    w_scales = quantised.tile([P, OUT_F], U8, name="w_scales", align_bytes=64)
+                    w_q[c] = (w_codes, w_scales)
+                cols = slice((pair - 1) * 2 * P, pair * 2 * P)
+                codes, scales = w_q[c][0][:, cols], w_q[c][1][:, cols]
+            nc.vector.quantize_mx(
+                out=codes.bitcast(FP8X4), scales=scales, in_=group_tiles[c, pair][:]
+            )
 
         def multiply(c):
-            x_q, w_q = codes[c]
             for mt in range(M_TILES):
                 rows = slice(mt * P, (mt + 1) * P)
                 nc.tensor.matmul_mx(
                     out=acc[mt][:],
-                    lhsT=x_q[0][:, rows].bitcast(FP8X4),
-                    lhsT_scale=x_q[1][:, rows],
-                    rhs=w_q[0][:].bitcast(FP8X4),
-                    rhs_scale=w_q[1][:],
+                    lhsT=x_q[c][0][:, rows].bitcast(FP8X4),
+                    lhsT_scale=x_q[c][1][:, rows],
+                    rhs=w_q[c][0][:].bitcast(FP8X4),
+                    rhs_scale=w_q[c][1][:],
                     start=(c == 0),
                     stop=(c == N_PASS - 1),
                 )
 
         ctx.enter_context(tc.manual_schedule())
+        to_permute = [item for item in items if item[1] == 0]
+        to_build = [item for item in items if item[1] > 0]
         multiplied = 0
-        free_step = {512: [2, 2], 1024: list(range(4, N_PASS, 2))}
-        for step in range(N_PASS + 3):
-            while len(chunks) < len(CHUNKS) and free_step[CHUNKS[len(chunks)]][0] <= step:
-                free_step[CHUNKS[len(chunks)]].pop(0)
-                load_chunk(len(chunks))
-            if step < N_PASS:
-                transpose_x(step)
-            if 0 <= step - 1 < N_PASS:
-                transpose_w(step - 1)
-            if step % MX_BATCH == 0 or step >= N_PASS:
-                while multiplied <= step - 3:
+        for slot in range(len(items) + QUANT_LAG):
+            while to_build and (
+                3 * (len(w_perms)) <= 2 * slot or to_build[0] in items[: slot + 2]
+            ):
+                if chunk_of_pass[to_build[0][0]][0] >= len(chunks):
+                    break
+                build(*to_build.pop(0))
+            while to_permute and to_permute[0] in items[: slot + 1 + PERMUTE_LEAD]:
+                permute_x(to_permute.pop(0)[0])
+            if slot < len(items):
+                transpose(*items[slot])
+            if slot >= QUANT_LAG:
+                quantise(*items[slot - QUANT_LAG])
+            if slot % PAIRS == PAIRS - 1 or slot >= len(items):
+                quantised_passes = [c for c, pair in items[: max(0, slot - QUANT_LAG - MX_LAG)] if pair == PAIR_ORDER[-1]]
+                limit = len(quantised_passes) if slot >= len(items) - 6 else min(len(quantised_passes), multiplied + 1)
+                while multiplied < limit:
                     multiply(multiplied)
                     multiplied += 1
-            if step < N_PASS:
-                build_weight(step)
-            if 0 <= step - 2 < N_PASS:
-                quantise(step - 2)
+            if len(chunks) < len(CHUNKS):
+                read = chunk_of_pass[items[min(slot, len(items) - 1)][0]][0]
+                built = chunk_of_pass[to_build[0][0]][0] if to_build else len(CHUNKS)
+                while len(chunks) < len(CHUNKS) and len(chunks) - CHUNKS_IN_SBUF < min(read, built):
+                    load_chunk()
+        while multiplied < N_PASS:
+            multiply(multiplied)
+            multiplied += 1
 
         for mt in range(M_TILES):
             result = results.tile([P, OUT_F], F32, name="result%d" % mt)
-            if mt == 0:
-                nc.vector.tensor_copy(out=result[:], in_=acc[mt][:])
-            else:
-                nc.scalar.copy(out=result[:], in_=acc[mt][:])
-            nc.sync.dma_start(out=out_rows[mt * P : (mt + 1) * P, :], in_=result[:])
+            copy = nc.vector.tensor_copy if mt == 0 else nc.scalar.copy
+            for half in range(2):
+                cols = slice(half * OUT_F // 2, (half + 1) * OUT_F // 2)
+                copy(
+                    out=result[:, cols].rearrange("p (n t) -> p n t", t=O_TILES),
+                    in_=acc[mt][:].rearrange("p (t n) -> p n t", t=O_TILES)[
+                        :, half * P // 2 : (half + 1) * P // 2, :
+                    ],
+                )
+                nc.sync.dma_start(out=out_rows[mt * P : (mt + 1) * P, cols], in_=result[:, cols])

@@ -139,23 +139,17 @@ def tile_signcondpackedbitlinear_k_kernel(tc, x, signs, scale_pos, scale_neg, gs
             chunk, first = chunk_of_pass[c]
             src = chunks[chunk][1][:, first : first + K_PASS]
             x_perm = permuted.tile([P, K_PASS], BF16, name="x_perm")
-            if c % 2 == 0:
-                nc.vector.tensor_copy(
-                    out=x_perm[:].rearrange("p (h w e) -> p h w e", h=2, e=2),
-                    in_=src.rearrange("p (w h e) -> p h w e", h=2, e=2),
-                )
-            else:
-                nc.scalar.copy(
-                    out=x_perm[:].bitcast(F32).rearrange("p (h w) -> p h w", h=2),
-                    in_=src.bitcast(F32).rearrange("p (w h) -> p h w", h=2),
-                )
+            nc.scalar.copy(
+                out=x_perm[:].bitcast(F32).rearrange("p (h w) -> p h w", h=2),
+                in_=src.bitcast(F32).rearrange("p (w h) -> p h w", h=2),
+            )
             x_perms[c] = x_perm
 
         def transpose(c, pair):
             bank = psum_t.tile([P, 2, 2 * P], F32, name="bank")
             for i in range(2):
                 for h in range(2):
-                    if pair == 0 and i == 0:
+                    if pair == 0 and (i == 0 or c % 2 == 0):
                         chunk, first = chunk_of_pass[c]
                         words = chunks[chunk][i][:, first : first + K_PASS].bitcast(F32)
                         in_words = words[:, h : 2 * P : 2]
@@ -203,7 +197,7 @@ def tile_signcondpackedbitlinear_k_kernel(tc, x, signs, scale_pos, scale_neg, gs
                 )
 
         ctx.enter_context(tc.manual_schedule())
-        to_permute = [item for item in items if item[1] == 0]
+        to_permute = [item for item in items if item[1] == 0 and item[0] % 2 == 1]
         to_build = [item for item in items if item[1] > 0]
         multiplied = 0
         for slot in range(len(items) + QUANT_LAG):

@@ -25,11 +25,13 @@ N_PASS = IN_F // K_PASS
 GROUPS_PER_PASS = K_PASS // GROUP
 CHUNKS = 16 * (1024,)
 CHUNKS_IN_SBUF = 9
+X_LOADS_IN_SBUF = 6
 MX_LAG = 0
 PERMUTE_LEAD = 2
 QUANT_LAG = 4
 PAIRS = 1 + O_TILES // 2
 PAIR_ORDER = (1, 0, 2)
+LAST_ORDER = (0, 1, 2)
 LOAD_ORDER = (2, 3, 0, 1, 4, 5)
 
 FLOPS = 2 * TOKENS * IN_F * OUT_F
@@ -57,22 +59,32 @@ def tile_signcondpackedbitlinear_k_kernel(tc, x, signs, scale_pos, scale_neg, gs
         for i, width in enumerate(CHUNKS):
             first_pass = sum(CHUNKS[:i]) // K_PASS
             passes = range(first_pass, first_pass + width // K_PASS)
-            items.extend((c, pair) for pair in PAIR_ORDER for c in passes)
+            order = LAST_ORDER if i == len(CHUNKS) - 1 else PAIR_ORDER
+            items.extend((c, pair) for pair in order for c in passes)
             chunk_of_pass.extend((i, (c - first_pass) * K_PASS) for c in passes)
         chunks = []
+        x_second = {}
 
         def load_chunk():
             i = len(chunks)
             cols = slice(sum(CHUNKS[:i]), sum(CHUNKS[: i + 1]))
             tiles = {}
             for rt in LOAD_ORDER:
-                tile_n = natural.tile([P, CHUNKS[i]], BF16, name="natural%d" % rt)
                 if rt < M_TILES:
-                    rows = x_rows[rt * P : (rt + 1) * P, cols]
+                    if i < 2 or i % 2 == 0:
+                        width = CHUNKS[i] if i < 2 else 2 * CHUNKS[i]
+                        x_tile = natural.tile([P, width], BF16, name="natural%d" % rt, bufs=X_LOADS_IN_SBUF)
+                        both = slice(cols.start, cols.start + width)
+                        nc.sync.dma_start(out=x_tile[:], in_=x_rows[rt * P : (rt + 1) * P, both])
+                        tiles[rt] = x_tile[:, 0 : CHUNKS[i]]
+                        if i >= 2:
+                            x_second[rt] = x_tile[:, CHUNKS[i] : width]
+                    else:
+                        tiles[rt] = x_second[rt]
                 else:
-                    rows = sign_rows[:, rt - M_TILES, cols]
-                nc.sync.dma_start(out=tile_n[:], in_=rows)
-                tiles[rt] = tile_n
+                    tile_s = natural.tile([P, CHUNKS[i]], BF16, name="natural%d" % rt)
+                    nc.sync.dma_start(out=tile_s[:], in_=sign_rows[:, rt - M_TILES, cols])
+                    tiles[rt] = tile_s
             chunks.append(tiles)
 
         pos = const.tile([P, O_TILES * GROUPS], BF16, name="pos")
@@ -89,8 +101,8 @@ def tile_signcondpackedbitlinear_k_kernel(tc, x, signs, scale_pos, scale_neg, gs
         half_neg = const.tile([P, O_TILES * GROUPS], F32, name="half_neg")
         slope = const.tile([P, O_TILES * GROUPS], F32, name="slope")
         offset = const.tile([P, O_TILES * GROUPS], F32, name="offset")
-        for ot in range(O_TILES):
-            cols = slice(ot * GROUPS, (ot + 1) * GROUPS)
+        def derive(pair):
+            cols = slice((pair - 1) * 2 * GROUPS, pair * 2 * GROUPS)
             nc.vector.tensor_scalar(
                 out=half_neg[:, cols], in0=neg[:, cols], scalar1=0.5, scalar2=None, op0=MULT
             )
@@ -106,6 +118,13 @@ def tile_signcondpackedbitlinear_k_kernel(tc, x, signs, scale_pos, scale_neg, gs
                 op1=SUBTRACT,
             )
 
+        derive(1)
+        cols2 = slice(2 * GROUPS, 4 * GROUPS)
+        half_pos = const.tile([P, 2 * GROUPS], F32, name="half_pos")
+        nc.gpsimd.tensor_scalar(out=half_neg[:, cols2], in0=neg[:, cols2], scalar1=0.5, scalar2=0.0, op0=MULT, op1=ADD)
+        nc.gpsimd.tensor_scalar(out=half_pos[:], in0=pos[:, cols2], scalar1=0.5, scalar2=0.0, op0=MULT, op1=ADD)
+        nc.gpsimd.tensor_tensor(out=slope[:, cols2], in0=half_pos[:], in1=half_neg[:, cols2], op=ADD)
+        nc.gpsimd.tensor_tensor(out=offset[:, cols2], in0=half_pos[:], in1=half_neg[:, cols2], op=SUBTRACT)
         acc = [psum_acc.tile([P, OUT_F], F32, name="acc%d" % mt) for mt in range(M_TILES)]
         x_perms = {}
         w_perms = {}

from contextlib import ExitStack

import concourse.mybir as mybir
from concourse.masks import make_identity

BF16 = mybir.dt.bfloat16
F32 = mybir.dt.float32
U32 = mybir.dt.uint32
U8 = mybir.dt.uint8
FP8X4 = mybir.dt.float8_e4m3fn_x4
MULT = mybir.AluOpType.mult
ADD = mybir.AluOpType.add
SUBTRACT = mybir.AluOpType.subtract

P = 128
TOKENS = 256
IN_F = 16384
OUT_F = 512
GROUP = 128
GROUPS = IN_F // GROUP
M_TILES = TOKENS // P
O_TILES = OUT_F // P
K_PASS = 4 * P
N_PASS = IN_F // K_PASS
GROUPS_PER_PASS = K_PASS // GROUP
CHUNKS = 16 * (1024,)
CHUNKS_IN_SBUF = 9
X_LOADS_IN_SBUF = 6
MX_LAG = 0
PERMUTE_LEAD = 2
QUANT_LAG = 4
PAIRS = 1 + O_TILES // 2
PAIR_ORDER = (1, 0, 2)
LAST_ORDER = (0, 1, 2)
LOAD_ORDER = (2, 3, 0, 1, 4, 5)

FLOPS = 2 * TOKENS * IN_F * OUT_F


def tile_signcondpackedbitlinear_k_kernel(tc, x, signs, scale_pos, scale_neg, gs, out):
    nc = tc.nc
    assert gs == GROUP
    x_rows = x.flatten_outer_dims()
    out_rows = out.flatten_outer_dims()
    sign_rows = signs.rearrange("(p t) k -> p t k", t=O_TILES)

    with ExitStack() as ctx:
        const = ctx.enter_context(tc.tile_pool(name="const", bufs=1))
        natural = ctx.enter_context(tc.tile_pool(name="natural", bufs=CHUNKS_IN_SBUF))
        permuted = ctx.enter_context(tc.tile_pool(name="permuted", bufs=8))
        grouped = ctx.enter_context(tc.tile_pool(name="grouped", bufs=8))
        quantised = ctx.enter_context(tc.tile_pool(name="quantised", bufs=8))
        results = ctx.enter_context(tc.tile_pool(name="results", bufs=1))
        psum_acc = ctx.enter_context(tc.psum_pool(name="psum_acc", bufs=1))
        psum_t = ctx.enter_context(tc.psum_pool(name="psum_t", bufs=6))

        items = []
        chunk_of_pass = []
        for i, width in enumerate(CHUNKS):
            first_pass = sum(CHUNKS[:i]) // K_PASS
            passes = range(first_pass, first_pass + width // K_PASS)
            order = LAST_ORDER if i == len(CHUNKS) - 1 else PAIR_ORDER
            items.extend((c, pair) for pair in order for c in passes)
            chunk_of_pass.extend((i, (c - first_pass) * K_PASS) for c in passes)
        chunks = []
        x_second = {}

        def load_chunk():
            i = len(chunks)
            cols = slice(sum(CHUNKS[:i]), sum(CHUNKS[: i + 1]))
            tiles = {}
            for rt in LOAD_ORDER:
                if rt < M_TILES:
                    if i < 2 or i % 2 == 0:
                        width = CHUNKS[i] if i < 2 else 2 * CHUNKS[i]
                        x_tile = natural.tile([P, width], BF16, name="natural%d" % rt, bufs=X_LOADS_IN_SBUF)
                        both = slice(cols.start, cols.start + width)
                        nc.sync.dma_start(out=x_tile[:], in_=x_rows[rt * P : (rt + 1) * P, both])
                        tiles[rt] = x_tile[:, 0 : CHUNKS[i]]
                        if i >= 2:
                            x_second[rt] = x_tile[:, CHUNKS[i] : width]
                    else:
                        tiles[rt] = x_second[rt]
                else:
                    tile_s = natural.tile([P, CHUNKS[i]], BF16, name="natural%d" % rt)
                    nc.sync.dma_start(out=tile_s[:], in_=sign_rows[:, rt - M_TILES, cols])
                    tiles[rt] = tile_s
            chunks.append(tiles)

        pos = const.tile([P, O_TILES * GROUPS], BF16, name="pos")
        neg = const.tile([P, O_TILES * GROUPS], BF16, name="neg")
        nc.sync.dma_start(out=pos[:], in_=scale_pos.rearrange("(p c) -> p c", p=P))
        nc.sync.dma_start(out=neg[:], in_=scale_neg.rearrange("(p c) -> p c", p=P))

        for i in range(CHUNKS_IN_SBUF):
            load_chunk()

        ident = const.tile([P, P], F32, name="ident")
        make_identity(nc, ident[:])

        half_neg = const.tile([P, O_TILES * GROUPS], F32, name="half_neg")
        slope = const.tile([P, O_TILES * GROUPS], F32, name="slope")
        offset = const.tile([P, O_TILES * GROUPS], F32, name="offset")
        def derive(pair):
            cols = slice((pair - 1) * 2 * GROUPS, pair * 2 * GROUPS)
            nc.vector.tensor_scalar(
                out=half_neg[:, cols], in0=neg[:, cols], scalar1=0.5, scalar2=None, op0=MULT
            )
            nc.vector.scalar_tensor_tensor(
                out=slope[:, cols], in0=pos[:, cols], scalar=0.5, in1=half_neg[:, cols], op0=MULT, op1=ADD
            )
            nc.vector.scalar_tensor_tensor(
                out=offset[:, cols],
                in0=pos[:, cols],
                scalar=0.5,
                in1=half_neg[:, cols],
                op0=MULT,
                op1=SUBTRACT,
            )

        derive(1)
        cols2 = slice(2 * GROUPS, 4 * GROUPS)
        half_pos = const.tile([P, 2 * GROUPS], F32, name="half_pos")
        nc.gpsimd.tensor_scalar(out=half_neg[:, cols2], in0=neg[:, cols2], scalar1=0.5, scalar2=0.0, op0=MULT, op1=ADD)
        nc.gpsimd.tensor_scalar(out=half_pos[:], in0=pos[:, cols2], scalar1=0.5, scalar2=0.0, op0=MULT, op1=ADD)
        nc.gpsimd.tensor_tensor(out=slope[:, cols2], in0=half_pos[:], in1=half_neg[:, cols2], op=ADD)
        nc.gpsimd.tensor_tensor(out=offset[:, cols2], in0=half_pos[:], in1=half_neg[:, cols2], op=SUBTRACT)
        acc = [psum_acc.tile([P, OUT_F], F32, name="acc%d" % mt) for mt in range(M_TILES)]
        x_perms = {}
        w_perms = {}
        group_tiles = {}
        x_q = {}
        w_q = {}

        def build(c, pair):
            chunk, first = chunk_of_pass[c]
            w_perm = permuted.tile([P, 2 * K_PASS], BF16, name="w_perm")
            for i in range(2):
                ot = 2 * (pair - 1) + i
                src_tile = chunks[chunk][M_TILES + ot]
                dst = w_perm[:, i * K_PASS : (i + 1) * K_PASS].rearrange(
                    "p (h j w) -> p h j w", h=2, j=GROUPS_PER_PASS
                )
                for j in range(GROUPS_PER_PASS):
                    g = ot * GROUPS + c * GROUPS_PER_PASS + j
                    src = src_tile[:, first + j * GROUP : first + (j + 1) * GROUP]
                    nc.vector.tensor_scalar(
                        out=dst[:, :, j, :].rearrange("p h (w e) -> p h w e", e=2),
                        in0=src.rearrange("p (w h e) -> p h w e", h=2, e=2),
                        scalar1=slope[:, g : g + 1],
                        scalar2=offset[:, g : g + 1],
                        op0=MULT,
                        op1=ADD,
                    )
            w_perms[c, pair] = w_perm

        def permute_x(c):
            chunk, first = chunk_of_pass[c]
            src = chunks[chunk][1][:, first : first + K_PASS]
            x_perm = permuted.tile([P, K_PASS], BF16, name="x_perm")
            nc.scalar.copy(
                out=x_perm[:].bitcast(F32).rearrange("p (h w) -> p h w", h=2),
                in_=src.bitcast(F32).rearrange("p (w h) -> p h w", h=2),
            )
            x_perms[c] = x_perm

        def transpose(c, pair):
            bank = psum_t.tile([P, 2, 2 * P], F32, name="bank")
            for i in range(2):
                for h in range(2):
                    if pair == 0 and (i == 0 or c % 2 == 0):
                        chunk, first = chunk_of_pass[c]
                        words = chunks[chunk][i][:, first : first + K_PASS].bitcast(F32)
                        in_words = words[:, h : 2 * P : 2]
                    elif pair == 0:
                        in_words = x_perms[c][:].bitcast(F32)[:, h * P : (h + 1) * P]
                    else:
                        words = w_perms[c, pair][:].bitcast(F32)
                        in_words = words[:, (2 * i + h) * P : (2 * i + h + 1) * P]
                    nc.tensor.transpose(bank[:, h, i * P : (i + 1) * P], in_words, ident[:])
            group_tile = grouped.tile([P, 2 * P * 4], BF16, name="group_tile", align_bytes=64)
            nc.scalar.copy(
                out=group_tile[:].bitcast(F32).rearrange("p (n h) -> p n h", h=2),
                in_=bank[:].rearrange("p h n -> p n h"),
            )
            group_tiles[c, pair] = group_tile

        def quantise(c, pair):
            if pair == 0:
                x_codes = quantised.tile([P, TOKENS], U32, name="x_codes", align_bytes=64)
                x_scales = quantised.tile([P, TOKENS], U8, name="x_scales", align_bytes=64)
                x_q[c] = (x_codes, x_scales)
                codes, scales = x_codes[:], x_scales[:]
            else:
                if c not in w_q:
                    w_codes = quantised.tile([P, OUT_F], U32, name="w_codes", align_bytes=64)
                    w_scales = quantised.tile([P, OUT_F], U8, name="w_scales", align_bytes=64)
                    w_q[c] = (w_codes, w_scales)
                cols = slice((pair - 1) * 2 * P, pair * 2 * P)
                codes, scales = w_q[c][0][:, cols], w_q[c][1][:, cols]
            nc.vector.quantize_mx(
                out=codes.bitcast(FP8X4), scales=scales, in_=group_tiles[c, pair][:]
            )

        def multiply(c):
            for mt in range(M_TILES):
                rows = slice(mt * P, (mt + 1) * P)
                nc.tensor.matmul_mx(
                    out=acc[mt][:],
                    lhsT=x_q[c][0][:, rows].bitcast(FP8X4),
                    lhsT_scale=x_q[c][1][:, rows],
                    rhs=w_q[c][0][:].bitcast(FP8X4),
                    rhs_scale=w_q[c][1][:],
                    start=(c == 0),
                    stop=(c == N_PASS - 1),
                )

        ctx.enter_context(tc.manual_schedule())
        to_permute = [item for item in items if item[1] == 0 and item[0] % 2 == 1]
        to_build = [item for item in items if item[1] > 0]
        multiplied = 0
        for slot in range(len(items) + QUANT_LAG):
            while to_build and (
                3 * (len(w_perms)) <= 2 * slot or to_build[0] in items[: slot + 2]
            ):
                if chunk_of_pass[to_build[0][0]][0] >= len(chunks):
                    break
                build(*to_build.pop(0))
            while to_permute and to_permute[0] in items[: slot + 1 + PERMUTE_LEAD]:
                permute_x(to_permute.pop(0)[0])
            if slot < len(items):
                transpose(*items[slot])
            if slot >= QUANT_LAG:
                quantise(*items[slot - QUANT_LAG])
            if slot % PAIRS == PAIRS - 1 or slot >= len(items):
                quantised_passes = [c for c, pair in items[: max(0, slot - QUANT_LAG - MX_LAG)] if pair == PAIR_ORDER[-1]]
                limit = len(quantised_passes) if slot >= len(items) - 6 else min(len(quantised_passes), multiplied + 1)
                while multiplied < limit:
                    multiply(multiplied)
                    multiplied += 1
            if len(chunks) < len(CHUNKS):
                read = chunk_of_pass[items[min(slot, len(items) - 1)][0]][0]
                built = chunk_of_pass[to_build[0][0]][0] if to_build else len(CHUNKS)
                while len(chunks) < len(CHUNKS) and len(chunks) - CHUNKS_IN_SBUF < min(read, built):
                    load_chunk()
        while multiplied < N_PASS:
            multiply(multiplied)
            multiplied += 1

        for mt in range(M_TILES):
            result = results.tile([P, OUT_F], F32, name="result%d" % mt)
            copy = nc.vector.tensor_copy if mt == 0 else nc.scalar.copy
            for half in range(2):
                cols = slice(half * OUT_F // 2, (half + 1) * OUT_F // 2)
                copy(
                    out=result[:, cols].rearrange("p (n t) -> p n t", t=O_TILES),
                    in_=acc[mt][:].rearrange("p (t n) -> p n t", t=O_TILES)[
                        :, half * P // 2 : (half + 1) * P // 2, :
                    ],
                )
                nc.sync.dma_start(out=out_rows[mt * P : (mt + 1) * P, cols], in_=result[:, cols])
